import numpy as np
import ml_dtypes


def mxq(x, axis, fmt="e4m3"):
    dtype, down = {"e4m3": (ml_dtypes.float8_e4m3fn, 7), "e5m2": (ml_dtypes.float8_e5m2, 14)}[fmt]
    v = np.moveaxis(np.asarray(x, np.float32).astype(ml_dtypes.bfloat16).astype(np.float64), axis, -1)
    blocks = v.reshape(v.shape[:-1] + (-1, 32))
    amax = np.abs(blocks).max(-1, keepdims=True)
    byte = np.maximum(np.where(amax > 0, np.frexp(amax)[1] - 1 + 127, 0) - down, 1)
    scale = np.exp2(byte - 127.0)
    codes = (blocks / scale).astype(np.float32).astype(dtype).astype(np.float64)
    return np.moveaxis((codes * scale).reshape(v.shape), -1, axis)


WIDE = False


def mx_kscale(k):
    if not WIDE:
        return np.ones(k)
    levels = np.array([10, -10, 5, -5, 0])
    a = np.random.permutation(np.resize(levels, k // 512 * 4)).reshape(k // 512, 4)
    idx = np.arange(k)
    return np.exp2(a[idx // 512, idx % 128 // 32])


BF16 = ml_dtypes.bfloat16


def bf(x):
    return np.asarray(x, np.float32).astype(BF16)


def f64(x):
    return np.asarray(x).astype(np.float64)


B, L, S, D, H = 2, 768, 768, 1024, 2
ITER = 3
E = D // H
QS = 1.4 / E ** 0.25


def setup_inputs():
    s = np.tile(mx_kscale(E), H)
    t = mx_kscale(D)
    q = (np.random.standard_normal((B, L, D)) + 0.35 * np.random.standard_normal(D)) * QS
    k = (np.random.standard_normal((B, S, D)) + 0.35 * np.random.standard_normal(D)) * QS
    return {"q_proj": bf(q * s), "k_proj": bf(k / s),
            "values": bf(np.random.standard_normal((B, S, D)) * t),
            "Wv": bf(np.random.standard_normal((D, D)) / np.sqrt(D) / t[:, None]),
            "bv": bf(np.random.standard_normal(D) * 0.2)}


def reference(q_proj, k_proj, values, Wv, bv):
    qh = mxq(f64(q_proj).reshape(B, L, H, E).transpose(0, 2, 1, 3), 3, "e4m3")
    kh = mxq(f64(k_proj).reshape(B, S, H, E).transpose(0, 2, 3, 1), 2, "e4m3")
    v = ((mxq(f64(values), 2, "e4m3") @ mxq(f64(Wv), 0, "e4m3")) + f64(bv)).reshape(B, S, H, E)
    attn_list = []
    acc = np.zeros((B, S, H, E))
    for i in range(ITER):
        stride = i + 1
        attn = qh[:, :, ::stride] @ kh
        attn_list.append(attn)
        e = np.exp(attn - attn.max(-1, keepdims=True))
        att = e / e.sum(-1, keepdims=True)
        colsum = att.sum(2)
        acc = acc + v * colsum.transpose(0, 2, 1)[..., None]
    return ((acc / ITER).reshape(B, S, D), *attn_list)

@@ -1,0 +1,345 @@
+from contextlib import ExitStack
+
+import concourse.mybir as mybir
+from concourse.masks import make_identity
+
+F32 = mybir.dt.float32
+BF16 = mybir.dt.bfloat16
+U32 = mybir.dt.uint32
+U8 = mybir.dt.uint8
+FP8X4 = mybir.dt.float8_e4m3fn_x4
+ALU = mybir.AluOpType
+ACT = mybir.ActivationFunctionType
+
+B, L, S, D, H = 2, 768, 768, 1024, 2
+E = D // H
+STRIDES = (1, 2, 3)
+
+P = 128
+PACK = 4
+K_PASS = P * PACK
+PASSES = D // K_PASS
+TILES = L // P
+PAIRS = TILES // 2
+BANK = 512
+REST = S - BANK
+
+assert E == K_PASS and E == BANK and L == S
+assert all(TILES % stride == 0 for stride in STRIDES)
+
+FLOPS = 2 * B * H * L * S * E + 2 * B * S * D * D
+
+
+def tile_trendattentionlayer_pa_kernel(
+    tc, q_proj, k_proj, values, Wv, bv, out_0, out_1, out_2, out_3
+):
+    nc = tc.nc
+    attn_out = {1: out_1, 2: out_2, 3: out_3}
+
+    with ExitStack() as ctx:
+        consts = ctx.enter_context(tc.tile_pool(name="consts", bufs=1))
+        raw = ctx.enter_context(tc.tile_pool(name="raw", bufs=B))
+        stage = ctx.enter_context(tc.tile_pool(name="stage", bufs=2))
+        mx = ctx.enter_context(tc.tile_pool(name="mx", bufs=2))
+        logit_pool = ctx.enter_context(tc.tile_pool(name="logit_pool", bufs=6))
+        expo_pool = ctx.enter_context(tc.tile_pool(name="expo_pool", bufs=4))
+        gated_pool = ctx.enter_context(tc.tile_pool(name="gated_pool", bufs=6))
+        small = ctx.enter_context(tc.tile_pool(name="small", bufs=4))
+        psum_two = ctx.enter_context(tc.psum_pool(name="psum_two", bufs=2))
+        psum_one = ctx.enter_context(tc.psum_pool(name="psum_one", bufs=1))
+        ctx.enter_context(tc.manual_schedule())
+
+        def load_rows(source, pattern, tag):
+            rows = raw.tile([P, TILES, D], BF16, tag=tag)
+            view = source.rearrange(pattern, p=P)
+            for pair in range(PAIRS):
+                piece = slice(2 * pair, 2 * pair + 2)
+                nc.sync.dma_start(out=rows[:, piece, :], in_=view[:, piece, :])
+            return rows
+
+        k_raw = [load_rows(k_proj[0], "(c p) d -> p c d", "k_raw")]
+        bias_rows = consts.tile([P, D], BF16)
+        nc.vector.memset(bias_rows[:], 0.0)
+        nc.sync.dma_start(out=bias_rows[0:1, :], in_=bv.rearrange("(o d) -> o d", o=1))
+        q_raw = [load_rows(q_proj[0], "(p r) d -> p r d", "q_raw")]
+        val_raw = [load_rows(values[0], "(c p) d -> p c d", "val_raw")]
+        wv_raw = consts.tile([P, PASSES, PACK, D], BF16)
+        nc.sync.dma_start(
+            out=wv_raw[:].rearrange("p g (u e) n -> p (g u) (e n)", e=2),
+            in_=Wv.rearrange("(q p e) n -> p q (e n)", p=P, e=2),
+        )
+        k_raw.append(load_rows(k_proj[1], "(c p) d -> p c d", "k_raw"))
+        q_raw.append(load_rows(q_proj[1], "(p r) d -> p r d", "q_raw"))
+        val_raw.append(load_rows(values[1], "(c p) d -> p c d", "val_raw"))
+
+        warm = consts.tile([P, 1], F32)
+        nc.vector.memset(warm[:], 0.0)
+        nc.scalar.activation(out=warm[:], in_=warm[:], func=ACT.Exp)
+        identity = consts.tile([P, P], F32)
+        make_identity(nc, identity[:])
+        ones = consts.tile([P, P], BF16)
+        nc.vector.memset(ones[:], 1.0)
+        stride_hits = consts.tile([P, TILES], F32)
+        for r in range(TILES):
+            hits = sum(1 for stride in STRIDES if r % stride == 0)
+            nc.vector.memset(stride_hits[:, r : r + 1], float(hits))
+        bias_all = consts.tile([P, D], F32)
+        wv_codes = consts.tile([P, PASSES, D], U32, align_bytes=64)
+        wv_scales = consts.tile([P, PASSES, D], U8, align_bytes=64)
+
+        def new_operand(tag):
+            codes = mx.tile([P, S], U32, tag=tag + "_codes", align_bytes=64)
+            scales = mx.tile([P, S], U8, tag=tag + "_scales", align_bytes=64)
+            return codes, scales
+
+        def turn_bank(rows, half, pair):
+            words = rows[:].bitcast(F32)
+            turned = psum_two.tile([P, 2, 2, P], F32, tag="turned")
+            for i in range(2):
+                for u in range(2):
+                    first = (K_PASS // 2) * half + P * u
+                    nc.tensor.transpose(
+                        turned[:, i, u, :], words[:, 2 * pair + i, first : first + P], identity[:]
+                    )
+            grouped = stage.tile([P, 2 * P, PACK], BF16, tag="grouped", bufs=6, align_bytes=64)
+            nc.scalar.copy(
+                out=grouped[:].bitcast(F32).rearrange("p (i r) u -> p i r u", i=2),
+                in_=turned[:].rearrange("p i u r -> p i r u"),
+            )
+            return grouped
+
+        def quantise_bank(grouped, operand, pair):
+            codes, scales = operand
+            cols = slice(2 * P * pair, 2 * P * (pair + 1))
+            nc.vector.quantize_mx(
+                out=codes[:, cols].bitcast(FP8X4),
+                scales=scales[:, cols],
+                in_=grouped[:].rearrange("p s t -> p (s t)"),
+            )
+
+        def regroup_wv(g, h):
+            wv_grouped = stage.tile([P, E, PACK], BF16, tag="wv_grouped", align_bytes=64)
+            nc.vector.tensor_copy(
+                out=wv_grouped[:].rearrange("p (c i) t -> p c t i", i=4),
+                in_=wv_raw[:, g, :, E * h : E * (h + 1)].rearrange("p t (c i) -> p c t i", i=4),
+            )
+            return wv_grouped
+
+        def quantise_wv(wv_grouped, g, h):
+            cols = slice(E * h, E * (h + 1))
+            nc.vector.quantize_mx(
+                out=wv_codes[:, g, cols].bitcast(FP8X4),
+                scales=wv_scales[:, g, cols],
+                in_=wv_grouped[:].rearrange("p n t -> p (n t)"),
+            )
+
+        def logit_matmuls(q_mx, k_mx, pair):
+            q_codes, q_scales = q_mx
+            k_codes, k_scales = k_mx
+            narrow = psum_one.tile([P, 2, REST], F32, tag="narrow")
+            wides = []
+            for i in range(2):
+                rows = slice(P * (2 * pair + i), P * (2 * pair + i + 1))
+                wide = psum_two.tile([P, BANK], F32, tag="wide")
+                wides.append(wide)
+                for target, cols in ((wide[:], slice(0, BANK)), (narrow[:, i, :], slice(BANK, S))):
+                    nc.tensor.matmul_mx(
+                        out=target,
+                        lhsT=q_codes[:, rows].bitcast(FP8X4),
+                        lhsT_scale=q_scales[:, rows],
+                        rhs=k_codes[:, cols].bitcast(FP8X4),
+                        rhs_scale=k_scales[:, cols],
+                        start=True,
+                        stop=True,
+                    )
+            return wides, narrow
+
+        def logits_out(wides, narrow):
+            logits = logit_pool.tile([P, 2, S], F32, tag="logits")
+            wide_max = small.tile([P, 2], F32, tag="wide_max")
+            row_max = small.tile([P, 2], F32, tag="row_max")
+            for i in range(2):
+                nc.vector.tensor_scalar(
+                    out=logits[:, i, 0:BANK], in0=wides[i][:], scalar1=1.0, scalar2=None,
+                    op0=ALU.mult, op1=ALU.max, accum_out=wide_max[:, i : i + 1],
+                )
+            for i in range(2):
+                nc.vector.tensor_scalar(
+                    out=logits[:, i, BANK:S], in0=narrow[:, i, :], scalar1=1.0,
+                    scalar2=wide_max[:, i : i + 1],
+                    op0=ALU.mult, op1=ALU.max, accum_out=row_max[:, i : i + 1],
+                )
+            neg_max = small.tile([P, 2], F32, tag="neg_max")
+            nc.vector.tensor_scalar_mul(out=neg_max[:], in0=row_max[:], scalar1=-1.0)
+            return logits, neg_max
+
+        def store_logits(b, h, pair, logits):
+            nc.sync.dma_start(
+                out=out_1[b, h].rearrange("(a r) s -> a r s", r=TILES)[:, 2 * pair : 2 * pair + 2, :],
+                in_=logits[:],
+            )
+            for stride in STRIDES[1:]:
+                for i in range(2):
+                    r = 2 * pair + i
+                    if r % stride == 0:
+                        nc.sync.dma_start(
+                            out=attn_out[stride][b, h].rearrange("(a m) s -> a m s", m=TILES // stride)[
+                                :, r // stride, :
+                            ],
+                            in_=logits[:, i, :],
+                        )
+
+        def exponentials(logits, neg_max):
+            row_sum = small.tile([P, 2], F32, tag="row_sum")
+            expos = []
+            for i in range(2):
+                expo = expo_pool.tile([P, S], F32, tag="expo")
+                expos.append(expo)
+                nc.scalar.activation(
+                    out=expo[:], in_=logits[:, i, :], func=ACT.Exp,
+                    bias=neg_max[:, i : i + 1], scale=1.0, accum_out=row_sum[:, i : i + 1],
+                )
+            return expos, row_sum
+
+        def row_weights(row_sum, pair):
+            inv_sum = small.tile([P, 2], F32, tag="inv_sum")
+            nc.vector.reciprocal(out=inv_sum[:], in_=row_sum[:])
+            row_weight = small.tile([P, 2], F32, tag="row_weight")
+            nc.vector.scalar_tensor_tensor(
+                out=row_weight[:], in0=inv_sum[:], scalar=1.0 / len(STRIDES),
+                in1=stride_hits[:, 2 * pair : 2 * pair + 2], op0=ALU.mult, op1=ALU.mult,
+            )
+            return row_weight
+
+        def column_sums(partial, pair, expos, row_weight):
+            for c in range(TILES):
+                for i in range(2):
+                    nc.tensor.matmul(
+                        out=partial[:, pair, c : c + 1],
+                        lhsT=expos[i][:, P * c : P * (c + 1)],
+                        rhs=row_weight[:, i : i + 1],
+                        start=(i == 0),
+                        stop=(i == 1),
+                    )
+
+        def value_matmuls(b, h, pair):
+            products = []
+            for c in (2 * pair, 2 * pair + 1):
+                rows = slice(P * c, P * (c + 1))
+                cols = slice(E * h, E * (h + 1))
+                acc = psum_two.tile([P, BANK], F32, tag="acc")
+                for g in range(PASSES):
+                    val_codes, val_scales = operands[("val", b, g)]
+                    nc.tensor.matmul_mx(
+                        out=acc[:],
+                        lhsT=val_codes[:, rows].bitcast(FP8X4),
+                        lhsT_scale=val_scales[:, rows],
+                        rhs=wv_codes[:, g, cols].bitcast(FP8X4),
+                        rhs_scale=wv_scales[:, g, cols],
+                        start=(g == 0),
+                        stop=(g == PASSES - 1),
+                    )
+                products.append((acc, b, h, c))
+            return products
+
+        def add_bias(products):
+            biased = []
+            for acc, b, h, c in products:
+                gated = gated_pool.tile([P, E], F32, tag="gated")
+                nc.vector.tensor_tensor(
+                    out=gated[:], in0=acc[:], in1=bias_all[:, E * h : E * (h + 1)], op=ALU.add
+                )
+                biased.append((gated, b, h, c))
+            return biased
+
+        def gate_and_store(biased):
+            for gated, b, h, c in biased:
+                nc.scalar.activation(
+                    out=gated[:], in_=gated[:], func=ACT.Copy, scale=col_sums[(b, h)][:, c : c + 1]
+                )
+                nc.sync.dma_start(
+                    out=out_0[b, P * c : P * (c + 1), E * h : E * (h + 1)], in_=gated[:]
+                )
+
+        operands = {}
+        col_sums = {}
+        sources = {"k": k_raw, "q": q_raw, "val": val_raw}
+
+        def operands_prepared_during(b, h):
+            if h + 1 < H:
+                return [("k", b, h + 1), ("q", b, h + 1)] + [("val", b, g) for g in range(PASSES)]
+            if b + 1 < B:
+                return [("k", b + 1, 0), ("q", b + 1, 0)]
+            return []
+
+        def operand_tag(key):
+            return key[0] if key[0] != "val" else "val%d" % key[2]
+
+        def close_head(partial, head):
+            col_sum = small.tile([P, TILES], F32, tag="col_sum")
+            nc.vector.tensor_reduce(
+                out=col_sum[:], in_=partial[:].rearrange("p k c -> p c k"),
+                axis=mybir.AxisListType.X, op=ALU.add,
+            )
+            col_sums[head] = col_sum
+
+        for key in (("k", 0, 0), ("q", 0, 0)):
+            operands[key] = new_operand(operand_tag(key))
+            for pair in range(PAIRS):
+                quantise_bank(turn_bank(sources[key[0]][0], 0, pair), operands[key], pair)
+            if key[0] == "k":
+                for h in range(H):
+                    cols = slice(E * h, E * (h + 1))
+                    spread = psum_two.tile([P, BANK], F32, tag="acc")
+                    nc.tensor.matmul(
+                        out=spread[:], lhsT=ones[:], rhs=bias_rows[:, cols], start=True, stop=True
+                    )
+                    nc.vector.tensor_copy(out=bias_all[:, cols], in_=spread[:])
+
+        lagging = None
+        partial = None
+        products = []
+        biased = []
+        gated_head = None
+        for b in range(B):
+            for h in range(H):
+                coming = operands_prepared_during(b, h)
+                for key in coming:
+                    operands[key] = new_operand(operand_tag(key))
+                for pair in range(PAIRS):
+                    gate_and_store(biased)
+                    biased = add_bias(products)
+                    wides, narrow = logit_matmuls(operands[("q", b, h)], operands[("k", b, h)], pair)
+                    logits, neg_max = logits_out(wides, narrow)
+                    store_logits(b, h, pair, logits)
+                    turned_banks = [turn_bank(sources[key[0]][key[1]], key[2], pair) for key in coming]
+                    products = value_matmuls(gated_head[0], gated_head[1], pair) if gated_head else []
+                    if lagging is not None:
+                        row_weight = row_weights(lagging[4], lagging[2])
+                        if lagging[2] == 0:
+                            partial = psum_one.tile([P, PAIRS, TILES], F32, tag="partial")
+                        column_sums(partial, lagging[2], lagging[3], row_weight)
+                    wv_pass = pair - 1
+                    if b == 0 and wv_pass >= 0:
+                        wv_grouped = regroup_wv(wv_pass, h)
+                    for key, grouped in zip(coming, turned_banks):
+                        quantise_bank(grouped, operands[key], pair)
+                    if b == 0 and wv_pass >= 0:
+                        quantise_wv(wv_grouped, wv_pass, h)
+                    if lagging is not None and lagging[2] == PAIRS - 1:
+                        close_head(partial, (lagging[0], lagging[1]))
+                    expos, row_sum = exponentials(logits, neg_max)
+                    lagging = (b, h, pair, expos, row_sum)
+                gated_head = (b, h)
+
+        gate_and_store(biased)
+        biased = add_bias(products)
+        products = value_matmuls(gated_head[0], gated_head[1], 0)
+        row_weight = row_weights(lagging[4], lagging[2])
+        column_sums(partial, lagging[2], lagging[3], row_weight)
+        close_head(partial, gated_head)
+        for pair in range(1, PAIRS + 1):
+            gate_and_store(biased)
+            biased = add_bias(products)
+            products = value_matmuls(gated_head[0], gated_head[1], pair) if pair < PAIRS else []
+        gate_and_store(biased)

@@ -23,6 +23,7 @@ TILES = L // P
 PAIRS = TILES // 2
 BANK = 512
 REST = S - BANK
+REPEAT = 16
 
 assert E == K_PASS and E == BANK and L == S
 assert all(TILES % stride == 0 for stride in STRIDES)
@@ -43,7 +44,8 @@ def tile_trendattentionlayer_pa_kernel(
         mx = ctx.enter_context(tc.tile_pool(name="mx", bufs=2))
         logit_pool = ctx.enter_context(tc.tile_pool(name="logit_pool", bufs=6))
         expo_pool = ctx.enter_context(tc.tile_pool(name="expo_pool", bufs=4))
-        gated_pool = ctx.enter_context(tc.tile_pool(name="gated_pool", bufs=6))
+        low_pool = ctx.enter_context(tc.tile_pool(name="low_pool", bufs=4))
+        gated_pool = ctx.enter_context(tc.tile_pool(name="gated_pool", bufs=10))
         small = ctx.enter_context(tc.tile_pool(name="small", bufs=4))
         psum_two = ctx.enter_context(tc.psum_pool(name="psum_two", bufs=2))
         psum_one = ctx.enter_context(tc.psum_pool(name="psum_one", bufs=1))
@@ -79,10 +81,10 @@ def tile_trendattentionlayer_pa_kernel(
         make_identity(nc, identity[:])
         ones = consts.tile([P, P], BF16)
         nc.vector.memset(ones[:], 1.0)
-        stride_hits = consts.tile([P, TILES], F32)
+        strides_per_hit = consts.tile([P, TILES], F32)
         for r in range(TILES):
             hits = sum(1 for stride in STRIDES if r % stride == 0)
-            nc.vector.memset(stride_hits[:, r : r + 1], float(hits))
+            nc.vector.memset(strides_per_hit[:, r : r + 1], len(STRIDES) / hits)
         bias_all = consts.tile([P, D], F32)
         wv_codes = consts.tile([P, PASSES, D], U32, align_bytes=64)
         wv_scales = consts.tile([P, PASSES, D], U8, align_bytes=64)
@@ -201,26 +203,58 @@ def tile_trendattentionlayer_pa_kernel(
                 )
             return expos, row_sum
 
-        def row_weights(row_sum, pair):
-            inv_sum = small.tile([P, 2], F32, tag="inv_sum")
-            nc.vector.reciprocal(out=inv_sum[:], in_=row_sum[:])
-            row_weight = small.tile([P, 2], F32, tag="row_weight")
-            nc.vector.scalar_tensor_tensor(
-                out=row_weight[:], in0=inv_sum[:], scalar=1.0 / len(STRIDES),
-                in1=stride_hits[:, 2 * pair : 2 * pair + 2], op0=ALU.mult, op1=ALU.mult,
-            )
-            return row_weight
+        def high_halves(expo):
+            return expo[:].bitcast(BF16).rearrange("p (s half) -> p s half", half=2)[:, :, 1]
 
-        def column_sums(partial, pair, expos, row_weight):
+        def low_parts(expos):
+            lows = []
+            for expo in expos:
+                low = low_pool.tile([P, S], BF16, tag="low")
+                lows.append(low)
+                nc.gpsimd.tensor_tensor(out=low[:], in0=expo[:], in1=high_halves(expo), op=ALU.subtract)
+            return lows
+
+        def row_weights(row_sum, pair):
+            scaled_sum = small.tile([P, 2], F32, tag="scaled_sum")
+            nc.vector.tensor_tensor(
+                out=scaled_sum[:], in0=row_sum[:], in1=strides_per_hit[:, 2 * pair : 2 * pair + 2], op=ALU.mult
+            )
+            weight = small.tile([P, 2], F32, tag="weight")
+            nc.vector.reciprocal(out=weight[:], in_=scaled_sum[:])
+            repeated = weight[:].unsqueeze(2).to_broadcast([P, 2, REPEAT])
+            pieces = small.tile([P, 2, 2, REPEAT], BF16, tag="pieces")
+            nc.vector.tensor_copy(out=pieces[:, :, 0, :], in_=repeated)
+            nc.vector.tensor_tensor(out=pieces[:, :, 1, :], in0=repeated, in1=pieces[:, :, 0, :], op=ALU.subtract)
+            return pieces
+
+        def column_sums(expos, lows, pieces):
+            partial = psum_one.tile([P, TILES, 2, REPEAT], F32, tag="partial")
             for c in range(TILES):
+                chunk = slice(P * c, P * (c + 1))
                 for i in range(2):
-                    nc.tensor.matmul(
-                        out=partial[:, pair, c : c + 1],
-                        lhsT=expos[i][:, P * c : P * (c + 1)],
-                        rhs=row_weight[:, i : i + 1],
-                        start=(i == 0),
-                        stop=(i == 1),
-                    )
+                    for part, stationary in enumerate((high_halves(expos[i])[:, chunk], lows[i][:, chunk])):
+                        nc.tensor.matmul(
+                            out=partial[:, c].rearrange("p w r -> p (w r)"),
+                            lhsT=stationary,
+                            rhs=pieces[:, i].rearrange("p w r -> p (w r)"),
+                            start=(i == 0 and part == 0),
+                            stop=(i == 1 and part == 1),
+                        )
+            return partial
+
+        def add_column_sums(partial, head, pair):
+            if pair == 0:
+                col_sums[head] = small.tile([P, TILES], F32, name="col_sum", tag="col_sum")
+                target = col_sums[head]
+            else:
+                target = small.tile([P, TILES], F32, name="pair_sum", tag="pair_sum")
+            nc.vector.tensor_reduce(
+                out=target[:], in_=partial[:, :, :, 0], axis=mybir.AxisListType.X, op=ALU.add
+            )
+            if pair > 0:
+                nc.vector.tensor_tensor(
+                    out=col_sums[head][:], in0=col_sums[head][:], in1=target[:], op=ALU.add
+                )
 
         def value_matmuls(b, h, pair):
             products = []
@@ -252,11 +286,13 @@ def tile_trendattentionlayer_pa_kernel(
                 biased.append((gated, b, h, c))
             return biased
 
-        def gate_and_store(biased):
+        def gate_and_store(biased, share_with_vector=False):
             for gated, b, h, c in biased:
-                nc.scalar.activation(
-                    out=gated[:], in_=gated[:], func=ACT.Copy, scale=col_sums[(b, h)][:, c : c + 1]
-                )
+                gate = col_sums[(b, h)][:, c : c + 1]
+                if share_with_vector and c % 2 == 1:
+                    nc.vector.tensor_scalar_mul(out=gated[:], in0=gated[:], scalar1=gate)
+                else:
+                    nc.scalar.activation(out=gated[:], in_=gated[:], func=ACT.Copy, scale=gate)
                 nc.sync.dma_start(
                     out=out_0[b, P * c : P * (c + 1), E * h : E * (h + 1)], in_=gated[:]
                 )
@@ -275,14 +311,6 @@ def tile_trendattentionlayer_pa_kernel(
         def operand_tag(key):
             return key[0] if key[0] != "val" else "val%d" % key[2]
 
-        def close_head(partial, head):
-            col_sum = small.tile([P, TILES], F32, tag="col_sum")
-            nc.vector.tensor_reduce(
-                out=col_sum[:], in_=partial[:].rearrange("p k c -> p c k"),
-                axis=mybir.AxisListType.X, op=ALU.add,
-            )
-            col_sums[head] = col_sum
-
         for key in (("k", 0, 0), ("q", 0, 0)):
             operands[key] = new_operand(operand_tag(key))
             for pair in range(PAIRS):
@@ -297,7 +325,7 @@ def tile_trendattentionlayer_pa_kernel(
                     nc.vector.tensor_copy(out=bias_all[:, cols], in_=spread[:])
 
         lagging = None
-        partial = None
+        summed = None
         products = []
         biased = []
         gated_head = None
@@ -308,6 +336,8 @@ def tile_trendattentionlayer_pa_kernel(
                     operands[key] = new_operand(operand_tag(key))
                 for pair in range(PAIRS):
                     gate_and_store(biased)
+                    if summed is not None:
+                        add_column_sums(summed[0], summed[1], summed[2])
                     biased = add_bias(products)
                     wides, narrow = logit_matmuls(operands[("q", b, h)], operands[("k", b, h)], pair)
                     logits, neg_max = logits_out(wides, narrow)
@@ -315,10 +345,10 @@ def tile_trendattentionlayer_pa_kernel(
                     turned_banks = [turn_bank(sources[key[0]][key[1]], key[2], pair) for key in coming]
                     products = value_matmuls(gated_head[0], gated_head[1], pair) if gated_head else []
                     if lagging is not None:
-                        row_weight = row_weights(lagging[4], lagging[2])
-                        if lagging[2] == 0:
-                            partial = psum_one.tile([P, PAIRS, TILES], F32, tag="partial")
-                        column_sums(partial, lagging[2], lagging[3], row_weight)
+                        pieces = row_weights(lagging[4], lagging[2])
+                        summed = (
+                            column_sums(lagging[3], lagging[5], pieces), (lagging[0], lagging[1]), lagging[2]
+                        )
                     wv_pass = pair - 1
                     if b == 0 and wv_pass >= 0:
                         wv_grouped = regroup_wv(wv_pass, h)
@@ -326,20 +356,16 @@ def tile_trendattentionlayer_pa_kernel(
                         quantise_bank(grouped, operands[key], pair)
                     if b == 0 and wv_pass >= 0:
                         quantise_wv(wv_grouped, wv_pass, h)
-                    if lagging is not None and lagging[2] == PAIRS - 1:
-                        close_head(partial, (lagging[0], lagging[1]))
                     expos, row_sum = exponentials(logits, neg_max)
-                    lagging = (b, h, pair, expos, row_sum)
+                    lagging = (b, h, pair, expos, row_sum, low_parts(expos))
                 gated_head = (b, h)
 
         gate_and_store(biased)
-        biased = add_bias(products)
-        products = value_matmuls(gated_head[0], gated_head[1], 0)
-        row_weight = row_weights(lagging[4], lagging[2])
-        column_sums(partial, lagging[2], lagging[3], row_weight)
-        close_head(partial, gated_head)
-        for pair in range(1, PAIRS + 1):
-            gate_and_store(biased)
-            biased = add_bias(products)
-            products = value_matmuls(gated_head[0], gated_head[1], pair) if pair < PAIRS else []
-        gate_and_store(biased)
+        add_column_sums(summed[0], summed[1], summed[2])
+        gate_and_store(add_bias(products))
+        pieces = row_weights(lagging[4], lagging[2])
+        biased = []
+        for pair in range(PAIRS):
+            biased.extend(add_bias(value_matmuls(gated_head[0], gated_head[1], pair)))
+        add_column_sums(column_sums(lagging[3], lagging[5], pieces), gated_head, lagging[2])
+        gate_and_store(biased, share_with_vector=True)

@@ -23,7 +23,7 @@ TILES = L // P
 PAIRS = TILES // 2
 BANK = 512
 REST = S - BANK
-REPEAT = 16
+REPEAT = 8
 
 assert E == K_PASS and E == BANK and L == S
 assert all(TILES % stride == 0 for stride in STRIDES)
@@ -81,10 +81,12 @@ def tile_trendattentionlayer_pa_kernel(
         make_identity(nc, identity[:])
         ones = consts.tile([P, P], BF16)
         nc.vector.memset(ones[:], 1.0)
-        strides_per_hit = consts.tile([P, TILES], F32)
+        stride_hits = consts.tile([P, TILES], F32)
         for r in range(TILES):
             hits = sum(1 for stride in STRIDES if r % stride == 0)
-            nc.vector.memset(strides_per_hit[:, r : r + 1], len(STRIDES) / hits)
+            nc.vector.memset(stride_hits[:, r : r + 1], float(hits))
+        hits_per_stride = consts.tile([P, TILES], F32)
+        nc.vector.tensor_scalar_mul(out=hits_per_stride[:], in0=stride_hits[:], scalar1=1.0 / len(STRIDES))
         bias_all = consts.tile([P, D], F32)
         wv_codes = consts.tile([P, PASSES, D], U32, align_bytes=64)
         wv_scales = consts.tile([P, PASSES, D], U8, align_bytes=64)
@@ -215,46 +217,38 @@ def tile_trendattentionlayer_pa_kernel(
             return lows
 
         def row_weights(row_sum, pair):
-            scaled_sum = small.tile([P, 2], F32, tag="scaled_sum")
-            nc.vector.tensor_tensor(
-                out=scaled_sum[:], in0=row_sum[:], in1=strides_per_hit[:, 2 * pair : 2 * pair + 2], op=ALU.mult
-            )
+            inv_sum = small.tile([P, 2], F32, tag="inv_sum")
+            nc.vector.reciprocal(out=inv_sum[:], in_=row_sum[:])
             weight = small.tile([P, 2], F32, tag="weight")
-            nc.vector.reciprocal(out=weight[:], in_=scaled_sum[:])
+            nc.gpsimd.tensor_tensor(
+                out=weight[:], in0=inv_sum[:], in1=hits_per_stride[:, 2 * pair : 2 * pair + 2], op=ALU.mult
+            )
             repeated = weight[:].unsqueeze(2).to_broadcast([P, 2, REPEAT])
             pieces = small.tile([P, 2, 2, REPEAT], BF16, tag="pieces")
-            nc.vector.tensor_copy(out=pieces[:, :, 0, :], in_=repeated)
-            nc.vector.tensor_tensor(out=pieces[:, :, 1, :], in0=repeated, in1=pieces[:, :, 0, :], op=ALU.subtract)
+            nc.gpsimd.tensor_scalar(
+                out=pieces[:, :, 0, :], in0=repeated, scalar1=1.0, scalar2=0.0, op0=ALU.mult, op1=ALU.add
+            )
+            nc.gpsimd.tensor_tensor(out=pieces[:, :, 1, :], in0=repeated, in1=pieces[:, :, 0, :], op=ALU.subtract)
             return pieces
 
-        def column_sums(expos, lows, pieces):
-            partial = psum_one.tile([P, TILES, 2, REPEAT], F32, tag="partial")
+        def column_sums(partial, pair, expos, lows, pieces):
             for c in range(TILES):
                 chunk = slice(P * c, P * (c + 1))
                 for i in range(2):
                     for part, stationary in enumerate((high_halves(expos[i])[:, chunk], lows[i][:, chunk])):
                         nc.tensor.matmul(
-                            out=partial[:, c].rearrange("p w r -> p (w r)"),
+                            out=partial[:, c, pair].rearrange("p w r -> p (w r)"),
                             lhsT=stationary,
                             rhs=pieces[:, i].rearrange("p w r -> p (w r)"),
                             start=(i == 0 and part == 0),
                             stop=(i == 1 and part == 1),
                         )
-            return partial
 
-        def add_column_sums(partial, head, pair):
-            if pair == 0:
-                col_sums[head] = small.tile([P, TILES], F32, name="col_sum", tag="col_sum")
-                target = col_sums[head]
-            else:
-                target = small.tile([P, TILES], F32, name="pair_sum", tag="pair_sum")
+        def close_head(partial, head):
+            col_sums[head] = small.tile([P, TILES], F32, name="col_sum", tag="col_sum")
             nc.vector.tensor_reduce(
-                out=target[:], in_=partial[:, :, :, 0], axis=mybir.AxisListType.X, op=ALU.add
+                out=col_sums[head][:], in_=partial[:, :, :, :, 0], axis=mybir.AxisListType.XY, op=ALU.add
             )
-            if pair > 0:
-                nc.vector.tensor_tensor(
-                    out=col_sums[head][:], in0=col_sums[head][:], in1=target[:], op=ALU.add
-                )
 
         def value_matmuls(b, h, pair):
             products = []
@@ -325,7 +319,8 @@ def tile_trendattentionlayer_pa_kernel(
                     nc.vector.tensor_copy(out=bias_all[:, cols], in_=spread[:])
 
         lagging = None
-        summed = None
+        partial = None
+        closing = None
         products = []
         biased = []
         gated_head = None
@@ -336,8 +331,9 @@ def tile_trendattentionlayer_pa_kernel(
                     operands[key] = new_operand(operand_tag(key))
                 for pair in range(PAIRS):
                     gate_and_store(biased)
-                    if summed is not None:
-                        add_column_sums(summed[0], summed[1], summed[2])
+                    if closing is not None:
+                        close_head(partial, closing)
+                        closing = None
                     biased = add_bias(products)
                     wides, narrow = logit_matmuls(operands[("q", b, h)], operands[("k", b, h)], pair)
                     logits, neg_max = logits_out(wides, narrow)
@@ -346,9 +342,11 @@ def tile_trendattentionlayer_pa_kernel(
                     products = value_matmuls(gated_head[0], gated_head[1], pair) if gated_head else []
                     if lagging is not None:
                         pieces = row_weights(lagging[4], lagging[2])
-                        summed = (
-                            column_sums(lagging[3], lagging[5], pieces), (lagging[0], lagging[1]), lagging[2]
-                        )
+                        if lagging[2] == 0:
+                            partial = psum_one.tile([P, TILES, PAIRS, 2, REPEAT], F32, tag="partial")
+                        column_sums(partial, lagging[2], lagging[3], lagging[5], pieces)
+                        if lagging[2] == PAIRS - 1:
+                            closing = (lagging[0], lagging[1])
                     wv_pass = pair - 1
                     if b == 0 and wv_pass >= 0:
                         wv_grouped = regroup_wv(wv_pass, h)
@@ -361,11 +359,11 @@ def tile_trendattentionlayer_pa_kernel(
                 gated_head = (b, h)
 
         gate_and_store(biased)
-        add_column_sums(summed[0], summed[1], summed[2])
         gate_and_store(add_bias(products))
         pieces = row_weights(lagging[4], lagging[2])
         biased = []
         for pair in range(PAIRS):
             biased.extend(add_bias(value_matmuls(gated_head[0], gated_head[1], pair)))
-        add_column_sums(column_sums(lagging[3], lagging[5], pieces), gated_head, lagging[2])
+        column_sums(partial, lagging[2], lagging[3], lagging[5], pieces)
+        close_head(partial, gated_head)
         gate_and_store(biased, share_with_vector=True)

@@ -335,13 +335,14 @@ def tile_trendattentionlayer_pa_kernel(
                         close_head(partial, closing)
                         closing = None
                     biased = add_bias(products)
+                    if lagging is not None:
+                        pieces = row_weights(lagging[4], lagging[2])
                     wides, narrow = logit_matmuls(operands[("q", b, h)], operands[("k", b, h)], pair)
                     logits, neg_max = logits_out(wides, narrow)
                     store_logits(b, h, pair, logits)
                     turned_banks = [turn_bank(sources[key[0]][key[1]], key[2], pair) for key in coming]
                     products = value_matmuls(gated_head[0], gated_head[1], pair) if gated_head else []
                     if lagging is not None:
-                        pieces = row_weights(lagging[4], lagging[2])
                         if lagging[2] == 0:
                             partial = psum_one.tile([P, TILES, PAIRS, 2, REPEAT], F32, tag="partial")
                         column_sums(partial, lagging[2], lagging[3], lagging[5], pieces)

@@ -48,31 +48,45 @@ def tile_trendattentionlayer_pa_kernel(
         gated_pool = ctx.enter_context(tc.tile_pool(name="gated_pool", bufs=10))
         small = ctx.enter_context(tc.tile_pool(name="small", bufs=4))
         psum_two = ctx.enter_context(tc.psum_pool(name="psum_two", bufs=2))
+        psum_side = ctx.enter_context(tc.psum_pool(name="psum_side", bufs=4))
         psum_one = ctx.enter_context(tc.psum_pool(name="psum_one", bufs=1))
         ctx.enter_context(tc.manual_schedule())
 
-        def load_rows(source, pattern, tag):
+        key_rows = "(c p) d -> p c d"
+        query_rows = "(p r) d -> p r d"
+
+        def new_rows(tag):
             rows = raw.tile([P, TILES, D], BF16, tag=tag)
-            view = source.rearrange(pattern, p=P)
-            for pair in range(PAIRS):
-                piece = slice(2 * pair, 2 * pair + 2)
-                nc.sync.dma_start(out=rows[:, piece, :], in_=view[:, piece, :])
             return rows
 
-        k_raw = [load_rows(k_proj[0], "(c p) d -> p c d", "k_raw")]
+        def load(rows, source, pattern, tiles, features):
+            nc.sync.dma_start(
+                out=rows[:, tiles, features], in_=source.rearrange(pattern, p=P)[:, tiles, features]
+            )
+
+        def load_in_pairs(rows, source, pattern):
+            for pair in range(PAIRS):
+                load(rows, source, pattern, slice(2 * pair, 2 * pair + 2), slice(0, D))
+
+        k_raw = [new_rows("k_raw") for b in range(B)]
+        q_raw = [new_rows("q_raw") for b in range(B)]
+        val_raw = [new_rows("val_raw") for b in range(B)]
         bias_rows = consts.tile([P, D], BF16)
         nc.vector.memset(bias_rows[:], 0.0)
-        nc.sync.dma_start(out=bias_rows[0:1, :], in_=bv.rearrange("(o d) -> o d", o=1))
-        q_raw = [load_rows(q_proj[0], "(p r) d -> p r d", "q_raw")]
-        val_raw = [load_rows(values[0], "(c p) d -> p c d", "val_raw")]
+        for h in range(H):
+            load(k_raw[0], k_proj[0], key_rows, slice(0, TILES), slice(E * h, E * (h + 1)))
+            load(q_raw[0], q_proj[0], query_rows, slice(0, TILES), slice(E * h, E * (h + 1)))
+            if h == 0:
+                nc.sync.dma_start(out=bias_rows[0:1, :], in_=bv.rearrange("(o d) -> o d", o=1))
+        load_in_pairs(val_raw[0], values[0], key_rows)
         wv_raw = consts.tile([P, PASSES, PACK, D], BF16)
         nc.sync.dma_start(
             out=wv_raw[:].rearrange("p g (u e) n -> p (g u) (e n)", e=2),
             in_=Wv.rearrange("(q p e) n -> p q (e n)", p=P, e=2),
         )
-        k_raw.append(load_rows(k_proj[1], "(c p) d -> p c d", "k_raw"))
-        q_raw.append(load_rows(q_proj[1], "(p r) d -> p r d", "q_raw"))
-        val_raw.append(load_rows(values[1], "(c p) d -> p c d", "val_raw"))
+        load_in_pairs(k_raw[1], k_proj[1], key_rows)
+        load_in_pairs(q_raw[1], q_proj[1], query_rows)
+        load_in_pairs(val_raw[1], values[1], key_rows)
 
         warm = consts.tile([P, 1], F32)
         nc.vector.memset(warm[:], 0.0)
@@ -96,9 +110,9 @@ def tile_trendattentionlayer_pa_kernel(
             scales = mx.tile([P, S], U8, tag=tag + "_scales", align_bytes=64)
             return codes, scales
 
-        def turn_bank(rows, half, pair):
+        def turn_bank(rows, half, pair, on_vector=False):
             words = rows[:].bitcast(F32)
-            turned = psum_two.tile([P, 2, 2, P], F32, tag="turned")
+            turned = psum_side.tile([P, 2, 2, P], F32, tag="side")
             for i in range(2):
                 for u in range(2):
                     first = (K_PASS // 2) * half + P * u
@@ -106,10 +120,11 @@ def tile_trendattentionlayer_pa_kernel(
                         turned[:, i, u, :], words[:, 2 * pair + i, first : first + P], identity[:]
                     )
             grouped = stage.tile([P, 2 * P, PACK], BF16, tag="grouped", bufs=6, align_bytes=64)
-            nc.scalar.copy(
-                out=grouped[:].bitcast(F32).rearrange("p (i r) u -> p i r u", i=2),
-                in_=turned[:].rearrange("p i u r -> p i r u"),
-            )
+            side_by_side = grouped[:].bitcast(F32).rearrange("p (i r) u -> p i r u", i=2)
+            if on_vector:
+                nc.vector.tensor_copy(out=side_by_side, in_=turned[:].rearrange("p i u r -> p i r u"))
+            else:
+                nc.scalar.copy(out=side_by_side, in_=turned[:].rearrange("p i u r -> p i r u"))
             return grouped
 
         def quantise_bank(grouped, operand, pair):
@@ -208,12 +223,13 @@ def tile_trendattentionlayer_pa_kernel(
         def high_halves(expo):
             return expo[:].bitcast(BF16).rearrange("p (s half) -> p s half", half=2)[:, :, 1]
 
-        def low_parts(expos):
+        def low_parts(expos, share_with_vector=False):
             lows = []
-            for expo in expos:
+            for i, expo in enumerate(expos):
                 low = low_pool.tile([P, S], BF16, tag="low")
                 lows.append(low)
-                nc.gpsimd.tensor_tensor(out=low[:], in0=expo[:], in1=high_halves(expo), op=ALU.subtract)
+                engine = nc.vector if share_with_vector and i == 1 else nc.gpsimd
+                engine.tensor_tensor(out=low[:], in0=expo[:], in1=high_halves(expo), op=ALU.subtract)
             return lows
 
         def row_weights(row_sum, pair):
@@ -255,7 +271,7 @@ def tile_trendattentionlayer_pa_kernel(
             for c in (2 * pair, 2 * pair + 1):
                 rows = slice(P * c, P * (c + 1))
                 cols = slice(E * h, E * (h + 1))
-                acc = psum_two.tile([P, BANK], F32, tag="acc")
+                acc = psum_side.tile([P, BANK], F32, tag="side")
                 for g in range(PASSES):
                     val_codes, val_scales = operands[("val", b, g)]
                     nc.tensor.matmul_mx(
@@ -312,7 +328,7 @@ def tile_trendattentionlayer_pa_kernel(
             if key[0] == "k":
                 for h in range(H):
                     cols = slice(E * h, E * (h + 1))
-                    spread = psum_two.tile([P, BANK], F32, tag="acc")
+                    spread = psum_side.tile([P, BANK], F32, tag="side")
                     nc.tensor.matmul(
                         out=spread[:], lhsT=ones[:], rhs=bias_rows[:, cols], start=True, stop=True
                     )
@@ -340,7 +356,10 @@ def tile_trendattentionlayer_pa_kernel(
                     wides, narrow = logit_matmuls(operands[("q", b, h)], operands[("k", b, h)], pair)
                     logits, neg_max = logits_out(wides, narrow)
                     store_logits(b, h, pair, logits)
-                    turned_banks = [turn_bank(sources[key[0]][key[1]], key[2], pair) for key in coming]
+                    turned_banks = [
+                        turn_bank(sources[key[0]][key[1]], key[2], pair, on_vector=(place == 3))
+                        for place, key in enumerate(coming)
+                    ]
                     products = value_matmuls(gated_head[0], gated_head[1], pair) if gated_head else []
                     if lagging is not None:
                         if lagging[2] == 0:
@@ -356,7 +375,8 @@ def tile_trendattentionlayer_pa_kernel(
                     if b == 0 and wv_pass >= 0:
                         quantise_wv(wv_grouped, wv_pass, h)
                     expos, row_sum = exponentials(logits, neg_max)
-                    lagging = (b, h, pair, expos, row_sum, low_parts(expos))
+                    last_slot = (b, h, pair) == (B - 1, H - 1, PAIRS - 1)
+                    lagging = (b, h, pair, expos, row_sum, low_parts(expos, share_with_vector=last_slot))
                 gated_head = (b, h)
 
         gate_and_store(biased)

@@ -23,7 +23,7 @@ TILES = L // P
 PAIRS = TILES // 2
 BANK = 512
 REST = S - BANK
-REPEAT = 8
+REPEAT = 24
 
 assert E == K_PASS and E == BANK and L == S
 assert all(TILES % stride == 0 for stride in STRIDES)
@@ -48,45 +48,31 @@ def tile_trendattentionlayer_pa_kernel(
         gated_pool = ctx.enter_context(tc.tile_pool(name="gated_pool", bufs=10))
         small = ctx.enter_context(tc.tile_pool(name="small", bufs=4))
         psum_two = ctx.enter_context(tc.psum_pool(name="psum_two", bufs=2))
-        psum_side = ctx.enter_context(tc.psum_pool(name="psum_side", bufs=4))
         psum_one = ctx.enter_context(tc.psum_pool(name="psum_one", bufs=1))
         ctx.enter_context(tc.manual_schedule())
 
-        key_rows = "(c p) d -> p c d"
-        query_rows = "(p r) d -> p r d"
-
-        def new_rows(tag):
+        def load_rows(source, pattern, tag):
             rows = raw.tile([P, TILES, D], BF16, tag=tag)
+            view = source.rearrange(pattern, p=P)
+            for pair in range(PAIRS):
+                piece = slice(2 * pair, 2 * pair + 2)
+                nc.sync.dma_start(out=rows[:, piece, :], in_=view[:, piece, :])
             return rows
 
-        def load(rows, source, pattern, tiles, features):
-            nc.sync.dma_start(
-                out=rows[:, tiles, features], in_=source.rearrange(pattern, p=P)[:, tiles, features]
-            )
-
-        def load_in_pairs(rows, source, pattern):
-            for pair in range(PAIRS):
-                load(rows, source, pattern, slice(2 * pair, 2 * pair + 2), slice(0, D))
-
-        k_raw = [new_rows("k_raw") for b in range(B)]
-        q_raw = [new_rows("q_raw") for b in range(B)]
-        val_raw = [new_rows("val_raw") for b in range(B)]
+        k_raw = [load_rows(k_proj[0], "(c p) d -> p c d", "k_raw")]
         bias_rows = consts.tile([P, D], BF16)
         nc.vector.memset(bias_rows[:], 0.0)
-        for h in range(H):
-            load(k_raw[0], k_proj[0], key_rows, slice(0, TILES), slice(E * h, E * (h + 1)))
-            load(q_raw[0], q_proj[0], query_rows, slice(0, TILES), slice(E * h, E * (h + 1)))
-            if h == 0:
-                nc.sync.dma_start(out=bias_rows[0:1, :], in_=bv.rearrange("(o d) -> o d", o=1))
-        load_in_pairs(val_raw[0], values[0], key_rows)
+        nc.sync.dma_start(out=bias_rows[0:1, :], in_=bv.rearrange("(o d) -> o d", o=1))
+        q_raw = [load_rows(q_proj[0], "(p r) d -> p r d", "q_raw")]
+        val_raw = [load_rows(values[0], "(c p) d -> p c d", "val_raw")]
         wv_raw = consts.tile([P, PASSES, PACK, D], BF16)
         nc.sync.dma_start(
             out=wv_raw[:].rearrange("p g (u e) n -> p (g u) (e n)", e=2),
             in_=Wv.rearrange("(q p e) n -> p q (e n)", p=P, e=2),
         )
-        load_in_pairs(k_raw[1], k_proj[1], key_rows)
-        load_in_pairs(q_raw[1], q_proj[1], query_rows)
-        load_in_pairs(val_raw[1], values[1], key_rows)
+        k_raw.append(load_rows(k_proj[1], "(c p) d -> p c d", "k_raw"))
+        q_raw.append(load_rows(q_proj[1], "(p r) d -> p r d", "q_raw"))
+        val_raw.append(load_rows(values[1], "(c p) d -> p c d", "val_raw"))
 
         warm = consts.tile([P, 1], F32)
         nc.vector.memset(warm[:], 0.0)
@@ -110,9 +96,9 @@ def tile_trendattentionlayer_pa_kernel(
             scales = mx.tile([P, S], U8, tag=tag + "_scales", align_bytes=64)
             return codes, scales
 
-        def turn_bank(rows, half, pair, on_vector=False):
+        def turn_bank(rows, half, pair):
             words = rows[:].bitcast(F32)
-            turned = psum_side.tile([P, 2, 2, P], F32, tag="side")
+            turned = psum_two.tile([P, 2, 2, P], F32, tag="turned")
             for i in range(2):
                 for u in range(2):
                     first = (K_PASS // 2) * half + P * u
@@ -120,11 +106,10 @@ def tile_trendattentionlayer_pa_kernel(
                         turned[:, i, u, :], words[:, 2 * pair + i, first : first + P], identity[:]
                     )
             grouped = stage.tile([P, 2 * P, PACK], BF16, tag="grouped", bufs=6, align_bytes=64)
-            side_by_side = grouped[:].bitcast(F32).rearrange("p (i r) u -> p i r u", i=2)
-            if on_vector:
-                nc.vector.tensor_copy(out=side_by_side, in_=turned[:].rearrange("p i u r -> p i r u"))
-            else:
-                nc.scalar.copy(out=side_by_side, in_=turned[:].rearrange("p i u r -> p i r u"))
+            nc.scalar.copy(
+                out=grouped[:].bitcast(F32).rearrange("p (i r) u -> p i r u", i=2),
+                in_=turned[:].rearrange("p i u r -> p i r u"),
+            )
             return grouped
 
         def quantise_bank(grouped, operand, pair):
@@ -223,13 +208,12 @@ def tile_trendattentionlayer_pa_kernel(
         def high_halves(expo):
             return expo[:].bitcast(BF16).rearrange("p (s half) -> p s half", half=2)[:, :, 1]
 
-        def low_parts(expos, share_with_vector=False):
+        def low_parts(expos):
             lows = []
-            for i, expo in enumerate(expos):
+            for expo in expos:
                 low = low_pool.tile([P, S], BF16, tag="low")
                 lows.append(low)
-                engine = nc.vector if share_with_vector and i == 1 else nc.gpsimd
-                engine.tensor_tensor(out=low[:], in0=expo[:], in1=high_halves(expo), op=ALU.subtract)
+                nc.gpsimd.tensor_tensor(out=low[:], in0=expo[:], in1=high_halves(expo), op=ALU.subtract)
             return lows
 
         def row_weights(row_sum, pair):
@@ -247,31 +231,41 @@ def tile_trendattentionlayer_pa_kernel(
             nc.gpsimd.tensor_tensor(out=pieces[:, :, 1, :], in0=repeated, in1=pieces[:, :, 0, :], op=ALU.subtract)
             return pieces
 
-        def column_sums(partial, pair, expos, lows, pieces):
+        def column_sums(expos, lows, pieces):
+            partial = psum_one.tile([P, TILES, 2, REPEAT], F32, tag="partial")
             for c in range(TILES):
                 chunk = slice(P * c, P * (c + 1))
                 for i in range(2):
                     for part, stationary in enumerate((high_halves(expos[i])[:, chunk], lows[i][:, chunk])):
                         nc.tensor.matmul(
-                            out=partial[:, c, pair].rearrange("p w r -> p (w r)"),
+                            out=partial[:, c].rearrange("p w r -> p (w r)"),
                             lhsT=stationary,
                             rhs=pieces[:, i].rearrange("p w r -> p (w r)"),
                             start=(i == 0 and part == 0),
                             stop=(i == 1 and part == 1),
                         )
+            return partial
 
-        def close_head(partial, head):
-            col_sums[head] = small.tile([P, TILES], F32, name="col_sum", tag="col_sum")
+        def add_column_sums(partial, head, pair):
+            if pair == 0:
+                col_sums[head] = small.tile([P, TILES], F32, name="col_sum", tag="col_sum")
+                target = col_sums[head]
+            else:
+                target = small.tile([P, TILES], F32, name="pair_sum", tag="pair_sum")
             nc.vector.tensor_reduce(
-                out=col_sums[head][:], in_=partial[:, :, :, :, 0], axis=mybir.AxisListType.XY, op=ALU.add
+                out=target[:], in_=partial[:, :, :, 0], axis=mybir.AxisListType.X, op=ALU.add
             )
+            if pair > 0:
+                nc.vector.tensor_tensor(
+                    out=col_sums[head][:], in0=col_sums[head][:], in1=target[:], op=ALU.add
+                )
 
         def value_matmuls(b, h, pair):
             products = []
             for c in (2 * pair, 2 * pair + 1):
                 rows = slice(P * c, P * (c + 1))
                 cols = slice(E * h, E * (h + 1))
-                acc = psum_side.tile([P, BANK], F32, tag="side")
+                acc = psum_two.tile([P, BANK], F32, tag="acc")
                 for g in range(PASSES):
                     val_codes, val_scales = operands[("val", b, g)]
                     nc.tensor.matmul_mx(
@@ -328,15 +322,14 @@ def tile_trendattentionlayer_pa_kernel(
             if key[0] == "k":
                 for h in range(H):
                     cols = slice(E * h, E * (h + 1))
-                    spread = psum_side.tile([P, BANK], F32, tag="side")
+                    spread = psum_two.tile([P, BANK], F32, tag="acc")
                     nc.tensor.matmul(
                         out=spread[:], lhsT=ones[:], rhs=bias_rows[:, cols], start=True, stop=True
                     )
                     nc.vector.tensor_copy(out=bias_all[:, cols], in_=spread[:])
 
         lagging = None
-        partial = None
-        closing = None
+        summed = None
         products = []
         biased = []
         gated_head = None
@@ -347,26 +340,20 @@ def tile_trendattentionlayer_pa_kernel(
                     operands[key] = new_operand(operand_tag(key))
                 for pair in range(PAIRS):
                     gate_and_store(biased)
-                    if closing is not None:
-                        close_head(partial, closing)
-                        closing = None
+                    if summed is not None:
+                        add_column_sums(summed[0], summed[1], summed[2])
                     biased = add_bias(products)
                     if lagging is not None:
                         pieces = row_weights(lagging[4], lagging[2])
                     wides, narrow = logit_matmuls(operands[("q", b, h)], operands[("k", b, h)], pair)
                     logits, neg_max = logits_out(wides, narrow)
                     store_logits(b, h, pair, logits)
-                    turned_banks = [
-                        turn_bank(sources[key[0]][key[1]], key[2], pair, on_vector=(place == 3))
-                        for place, key in enumerate(coming)
-                    ]
+                    turned_banks = [turn_bank(sources[key[0]][key[1]], key[2], pair) for key in coming]
                     products = value_matmuls(gated_head[0], gated_head[1], pair) if gated_head else []
                     if lagging is not None:
-                        if lagging[2] == 0:
-                            partial = psum_one.tile([P, TILES, PAIRS, 2, REPEAT], F32, tag="partial")
-                        column_sums(partial, lagging[2], lagging[3], lagging[5], pieces)
-                        if lagging[2] == PAIRS - 1:
-                            closing = (lagging[0], lagging[1])
+                        summed = (
+                            column_sums(lagging[3], lagging[5], pieces), (lagging[0], lagging[1]), lagging[2]
+                        )
                     wv_pass = pair - 1
                     if b == 0 and wv_pass >= 0:
                         wv_grouped = regroup_wv(wv_pass, h)
@@ -375,16 +362,15 @@ def tile_trendattentionlayer_pa_kernel(
                     if b == 0 and wv_pass >= 0:
                         quantise_wv(wv_grouped, wv_pass, h)
                     expos, row_sum = exponentials(logits, neg_max)
-                    last_slot = (b, h, pair) == (B - 1, H - 1, PAIRS - 1)
-                    lagging = (b, h, pair, expos, row_sum, low_parts(expos, share_with_vector=last_slot))
+                    lagging = (b, h, pair, expos, row_sum, low_parts(expos))
                 gated_head = (b, h)
 
         gate_and_store(biased)
+        add_column_sums(summed[0], summed[1], summed[2])
         gate_and_store(add_bias(products))
         pieces = row_weights(lagging[4], lagging[2])
         biased = []
         for pair in range(PAIRS):
             biased.extend(add_bias(value_matmuls(gated_head[0], gated_head[1], pair)))
-        column_sums(partial, lagging[2], lagging[3], lagging[5], pieces)
-        close_head(partial, gated_head)
+        add_column_sums(column_sums(lagging[3], lagging[5], pieces), gated_head, lagging[2])
         gate_and_store(biased, share_with_vector=True)

from contextlib import ExitStack

import concourse.mybir as mybir
from concourse.masks import make_identity

F32 = mybir.dt.float32
BF16 = mybir.dt.bfloat16
U32 = mybir.dt.uint32
U8 = mybir.dt.uint8
FP8X4 = mybir.dt.float8_e4m3fn_x4
ALU = mybir.AluOpType
ACT = mybir.ActivationFunctionType

B, L, S, D, H = 2, 768, 768, 1024, 2
E = D // H
STRIDES = (1, 2, 3)

P = 128
PACK = 4
K_PASS = P * PACK
PASSES = D // K_PASS
TILES = L // P
PAIRS = TILES // 2
BANK = 512
REST = S - BANK
REPEAT = 24

assert E == K_PASS and E == BANK and L == S
assert all(TILES % stride == 0 for stride in STRIDES)

FLOPS = 2 * B * H * L * S * E + 2 * B * S * D * D


def tile_trendattentionlayer_pa_kernel(
    tc, q_proj, k_proj, values, Wv, bv, out_0, out_1, out_2, out_3
):
    nc = tc.nc
    attn_out = {1: out_1, 2: out_2, 3: out_3}

    with ExitStack() as ctx:
        consts = ctx.enter_context(tc.tile_pool(name="consts", bufs=1))
        raw = ctx.enter_context(tc.tile_pool(name="raw", bufs=B))
        stage = ctx.enter_context(tc.tile_pool(name="stage", bufs=2))
        mx = ctx.enter_context(tc.tile_pool(name="mx", bufs=2))
        logit_pool = ctx.enter_context(tc.tile_pool(name="logit_pool", bufs=6))
        expo_pool = ctx.enter_context(tc.tile_pool(name="expo_pool", bufs=4))
        low_pool = ctx.enter_context(tc.tile_pool(name="low_pool", bufs=4))
        gated_pool = ctx.enter_context(tc.tile_pool(name="gated_pool", bufs=10))
        small = ctx.enter_context(tc.tile_pool(name="small", bufs=4))
        psum_two = ctx.enter_context(tc.psum_pool(name="psum_two", bufs=2))
        psum_one = ctx.enter_context(tc.psum_pool(name="psum_one", bufs=1))
        ctx.enter_context(tc.manual_schedule())

        def load_rows(source, pattern, tag):
            rows = raw.tile([P, TILES, D], BF16, tag=tag)
            view = source.rearrange(pattern, p=P)
            for pair in range(PAIRS):
                piece = slice(2 * pair, 2 * pair + 2)
                nc.sync.dma_start(out=rows[:, piece, :], in_=view[:, piece, :])
            return rows

        k_raw = [load_rows(k_proj[0], "(c p) d -> p c d", "k_raw")]
        bias_rows = consts.tile([P, D], BF16)
        nc.vector.memset(bias_rows[:], 0.0)
        nc.sync.dma_start(out=bias_rows[0:1, :], in_=bv.rearrange("(o d) -> o d", o=1))
        q_raw = [load_rows(q_proj[0], "(p r) d -> p r d", "q_raw")]
        val_raw = [load_rows(values[0], "(c p) d -> p c d", "val_raw")]
        wv_raw = consts.tile([P, PASSES, PACK, D], BF16)
        nc.sync.dma_start(
            out=wv_raw[:].rearrange("p g (u e) n -> p (g u) (e n)", e=2),
            in_=Wv.rearrange("(q p e) n -> p q (e n)", p=P, e=2),
        )
        k_raw.append(load_rows(k_proj[1], "(c p) d -> p c d", "k_raw"))
        q_raw.append(load_rows(q_proj[1], "(p r) d -> p r d", "q_raw"))
        val_raw.append(load_rows(values[1], "(c p) d -> p c d", "val_raw"))

        warm = consts.tile([P, 1], F32)
        nc.vector.memset(warm[:], 0.0)
        nc.scalar.activation(out=warm[:], in_=warm[:], func=ACT.Exp)
        identity = consts.tile([P, P], F32)
        make_identity(nc, identity[:])
        ones = consts.tile([P, P], BF16)
        nc.vector.memset(ones[:], 1.0)
        stride_hits = consts.tile([P, TILES], F32)
        for r in range(TILES):
            hits = sum(1 for stride in STRIDES if r % stride == 0)
            nc.vector.memset(stride_hits[:, r : r + 1], float(hits))
        hits_per_stride = consts.tile([P, TILES], F32)
        nc.vector.tensor_scalar_mul(out=hits_per_stride[:], in0=stride_hits[:], scalar1=1.0 / len(STRIDES))
        bias_all = consts.tile([P, D], F32)
        wv_codes = consts.tile([P, PASSES, D], U32, align_bytes=64)
        wv_scales = consts.tile([P, PASSES, D], U8, align_bytes=64)

        def new_operand(tag):
            codes = mx.tile([P, S], U32, tag=tag + "_codes", align_bytes=64)
            scales = mx.tile([P, S], U8, tag=tag + "_scales", align_bytes=64)
            return codes, scales

        def turn_bank(rows, half, pair):
            words = rows[:].bitcast(F32)
            turned = psum_two.tile([P, 2, 2, P], F32, tag="turned")
            for i in range(2):
                for u in range(2):
                    first = (K_PASS // 2) * half + P * u
                    nc.tensor.transpose(
                        turned[:, i, u, :], words[:, 2 * pair + i, first : first + P], identity[:]
                    )
            grouped = stage.tile([P, 2 * P, PACK], BF16, tag="grouped", bufs=6, align_bytes=64)
            nc.scalar.copy(
                out=grouped[:].bitcast(F32).rearrange("p (i r) u -> p i r u", i=2),
                in_=turned[:].rearrange("p i u r -> p i r u"),
            )
            return grouped

        def quantise_bank(grouped, operand, pair):
            codes, scales = operand
            cols = slice(2 * P * pair, 2 * P * (pair + 1))
            nc.vector.quantize_mx(
                out=codes[:, cols].bitcast(FP8X4),
                scales=scales[:, cols],
                in_=grouped[:].rearrange("p s t -> p (s t)"),
            )

        def regroup_wv(g, h):
            wv_grouped = stage.tile([P, E, PACK], BF16, tag="wv_grouped", align_bytes=64)
            nc.vector.tensor_copy(
                out=wv_grouped[:].rearrange("p (c i) t -> p c t i", i=4),
                in_=wv_raw[:, g, :, E * h : E * (h + 1)].rearrange("p t (c i) -> p c t i", i=4),
            )
            return wv_grouped

        def quantise_wv(wv_grouped, g, h):
            cols = slice(E * h, E * (h + 1))
            nc.vector.quantize_mx(
                out=wv_codes[:, g, cols].bitcast(FP8X4),
                scales=wv_scales[:, g, cols],
                in_=wv_grouped[:].rearrange("p n t -> p (n t)"),
            )

        def logit_matmuls(q_mx, k_mx, pair):
            q_codes, q_scales = q_mx
            k_codes, k_scales = k_mx
            narrow = psum_one.tile([P, 2, REST], F32, tag="narrow")
            wides = []
            for i in range(2):
                rows = slice(P * (2 * pair + i), P * (2 * pair + i + 1))
                wide = psum_two.tile([P, BANK], F32, tag="wide")
                wides.append(wide)
                for target, cols in ((wide[:], slice(0, BANK)), (narrow[:, i, :], slice(BANK, S))):
                    nc.tensor.matmul_mx(
                        out=target,
                        lhsT=q_codes[:, rows].bitcast(FP8X4),
                        lhsT_scale=q_scales[:, rows],
                        rhs=k_codes[:, cols].bitcast(FP8X4),
                        rhs_scale=k_scales[:, cols],
                        start=True,
                        stop=True,
                    )
            return wides, narrow

        def logits_out(wides, narrow):
            logits = logit_pool.tile([P, 2, S], F32, tag="logits")
            wide_max = small.tile([P, 2], F32, tag="wide_max")
            row_max = small.tile([P, 2], F32, tag="row_max")
            for i in range(2):
                nc.vector.tensor_scalar(
                    out=logits[:, i, 0:BANK], in0=wides[i][:], scalar1=1.0, scalar2=None,
                    op0=ALU.mult, op1=ALU.max, accum_out=wide_max[:, i : i + 1],
                )
            for i in range(2):
                nc.vector.tensor_scalar(
                    out=logits[:, i, BANK:S], in0=narrow[:, i, :], scalar1=1.0,
                    scalar2=wide_max[:, i : i + 1],
                    op0=ALU.mult, op1=ALU.max, accum_out=row_max[:, i : i + 1],
                )
            neg_max = small.tile([P, 2], F32, tag="neg_max")
            nc.vector.tensor_scalar_mul(out=neg_max[:], in0=row_max[:], scalar1=-1.0)
            return logits, neg_max

        def store_logits(b, h, pair, logits):
            nc.sync.dma_start(
                out=out_1[b, h].rearrange("(a r) s -> a r s", r=TILES)[:, 2 * pair : 2 * pair + 2, :],
                in_=logits[:],
            )
            for stride in STRIDES[1:]:
                for i in range(2):
                    r = 2 * pair + i
                    if r % stride == 0:
                        nc.sync.dma_start(
                            out=attn_out[stride][b, h].rearrange("(a m) s -> a m s", m=TILES // stride)[
                                :, r // stride, :
                            ],
                            in_=logits[:, i, :],
                        )

        def exponentials(logits, neg_max):
            row_sum = small.tile([P, 2], F32, tag="row_sum")
            expos = []
            for i in range(2):
                expo = expo_pool.tile([P, S], F32, tag="expo")
                expos.append(expo)
                nc.scalar.activation(
                    out=expo[:], in_=logits[:, i, :], func=ACT.Exp,
                    bias=neg_max[:, i : i + 1], scale=1.0, accum_out=row_sum[:, i : i + 1],
                )
            return expos, row_sum

        def high_halves(expo):
            return expo[:].bitcast(BF16).rearrange("p (s half) -> p s half", half=2)[:, :, 1]

        def low_parts(expos):
            lows = []
            for expo in expos:
                low = low_pool.tile([P, S], BF16, tag="low")
                lows.append(low)
                nc.gpsimd.tensor_tensor(out=low[:], in0=expo[:], in1=high_halves(expo), op=ALU.subtract)
            return lows

        def row_weights(row_sum, pair):
            inv_sum = small.tile([P, 2], F32, tag="inv_sum")
            nc.vector.reciprocal(out=inv_sum[:], in_=row_sum[:])
            weight = small.tile([P, 2], F32, tag="weight")
            nc.gpsimd.tensor_tensor(
                out=weight[:], in0=inv_sum[:], in1=hits_per_stride[:, 2 * pair : 2 * pair + 2], op=ALU.mult
            )
            repeated = weight[:].unsqueeze(2).to_broadcast([P, 2, REPEAT])
            pieces = small.tile([P, 2, 2, REPEAT], BF16, tag="pieces")
            nc.gpsimd.tensor_scalar(
                out=pieces[:, :, 0, :], in0=repeated, scalar1=1.0, scalar2=0.0, op0=ALU.mult, op1=ALU.add
            )
            nc.gpsimd.tensor_tensor(out=pieces[:, :, 1, :], in0=repeated, in1=pieces[:, :, 0, :], op=ALU.subtract)
            return pieces

        def column_sums(expos, lows, pieces):
            partial = psum_one.tile([P, TILES, 2, REPEAT], F32, tag="partial")
            for c in range(TILES):
                chunk = slice(P * c, P * (c + 1))
                for i in range(2):
                    for part, stationary in enumerate((high_halves(expos[i])[:, chunk], lows[i][:, chunk])):
                        nc.tensor.matmul(
                            out=partial[:, c].rearrange("p w r -> p (w r)"),
                            lhsT=stationary,
                            rhs=pieces[:, i].rearrange("p w r -> p (w r)"),
                            start=(i == 0 and part == 0),
                            stop=(i == 1 and part == 1),
                        )
            return partial

        def add_column_sums(partial, head, pair):
            if pair == 0:
                col_sums[head] = small.tile([P, TILES], F32, name="col_sum", tag="col_sum")
                target = col_sums[head]
            else:
                target = small.tile([P, TILES], F32, name="pair_sum", tag="pair_sum")
            nc.vector.tensor_reduce(
                out=target[:], in_=partial[:, :, :, 0], axis=mybir.AxisListType.X, op=ALU.add
            )
            if pair > 0:
                nc.vector.tensor_tensor(
                    out=col_sums[head][:], in0=col_sums[head][:], in1=target[:], op=ALU.add
                )

        def value_matmuls(b, h, pair):
            products = []
            for c in (2 * pair, 2 * pair + 1):
                rows = slice(P * c, P * (c + 1))
                cols = slice(E * h, E * (h + 1))
                acc = psum_two.tile([P, BANK], F32, tag="acc")
                for g in range(PASSES):
                    val_codes, val_scales = operands[("val", b, g)]
                    nc.tensor.matmul_mx(
                        out=acc[:],
                        lhsT=val_codes[:, rows].bitcast(FP8X4),
                        lhsT_scale=val_scales[:, rows],
                        rhs=wv_codes[:, g, cols].bitcast(FP8X4),
                        rhs_scale=wv_scales[:, g, cols],
                        start=(g == 0),
                        stop=(g == PASSES - 1),
                    )
                products.append((acc, b, h, c))
            return products

        def add_bias(products):
            biased = []
            for acc, b, h, c in products:
                gated = gated_pool.tile([P, E], F32, tag="gated")
                nc.vector.tensor_tensor(
                    out=gated[:], in0=acc[:], in1=bias_all[:, E * h : E * (h + 1)], op=ALU.add
                )
                biased.append((gated, b, h, c))
            return biased

        def gate_and_store(biased, share_with_vector=False):
            for gated, b, h, c in biased:
                gate = col_sums[(b, h)][:, c : c + 1]
                if share_with_vector and c % 2 == 1:
                    nc.vector.tensor_scalar_mul(out=gated[:], in0=gated[:], scalar1=gate)
                else:
                    nc.scalar.activation(out=gated[:], in_=gated[:], func=ACT.Copy, scale=gate)
                nc.sync.dma_start(
                    out=out_0[b, P * c : P * (c + 1), E * h : E * (h + 1)], in_=gated[:]
                )

        operands = {}
        col_sums = {}
        sources = {"k": k_raw, "q": q_raw, "val": val_raw}

        def operands_prepared_during(b, h):
            if h + 1 < H:
                return [("k", b, h + 1), ("q", b, h + 1)] + [("val", b, g) for g in range(PASSES)]
            if b + 1 < B:
                return [("k", b + 1, 0), ("q", b + 1, 0)]
            return []

        def operand_tag(key):
            return key[0] if key[0] != "val" else "val%d" % key[2]

        for key in (("k", 0, 0), ("q", 0, 0)):
            operands[key] = new_operand(operand_tag(key))
            for pair in range(PAIRS):
                quantise_bank(turn_bank(sources[key[0]][0], 0, pair), operands[key], pair)
            if key[0] == "k":
                for h in range(H):
                    cols = slice(E * h, E * (h + 1))
                    spread = psum_two.tile([P, BANK], F32, tag="acc")
                    nc.tensor.matmul(
                        out=spread[:], lhsT=ones[:], rhs=bias_rows[:, cols], start=True, stop=True
                    )
                    nc.vector.tensor_copy(out=bias_all[:, cols], in_=spread[:])

        lagging = None
        summed = None
        products = []
        biased = []
        gated_head = None
        for b in range(B):
            for h in range(H):
                coming = operands_prepared_during(b, h)
                for key in coming:
                    operands[key] = new_operand(operand_tag(key))
                for pair in range(PAIRS):
                    gate_and_store(biased)
                    if summed is not None:
                        add_column_sums(summed[0], summed[1], summed[2])
                    biased = add_bias(products)
                    if lagging is not None:
                        pieces = row_weights(lagging[4], lagging[2])
                    wides, narrow = logit_matmuls(operands[("q", b, h)], operands[("k", b, h)], pair)
                    logits, neg_max = logits_out(wides, narrow)
                    store_logits(b, h, pair, logits)
                    turned_banks = [turn_bank(sources[key[0]][key[1]], key[2], pair) for key in coming]
                    products = value_matmuls(gated_head[0], gated_head[1], pair) if gated_head else []
                    if lagging is not None:
                        summed = (
                            column_sums(lagging[3], lagging[5], pieces), (lagging[0], lagging[1]), lagging[2]
                        )
                    wv_pass = pair - 1
                    if b == 0 and wv_pass >= 0:
                        wv_grouped = regroup_wv(wv_pass, h)
                    for key, grouped in zip(coming, turned_banks):
                        quantise_bank(grouped, operands[key], pair)
                    if b == 0 and wv_pass >= 0:
                        quantise_wv(wv_grouped, wv_pass, h)
                    expos, row_sum = exponentials(logits, neg_max)
                    lagging = (b, h, pair, expos, row_sum, low_parts(expos))
                gated_head = (b, h)

        gate_and_store(biased)
        add_column_sums(summed[0], summed[1], summed[2])
        gate_and_store(add_bias(products))
        pieces = row_weights(lagging[4], lagging[2])
        biased = []
        for pair in range(PAIRS):
            biased.extend(add_bias(value_matmuls(gated_head[0], gated_head[1], pair)))
        add_column_sums(column_sums(lagging[3], lagging[5], pieces), gated_head, lagging[2])
        gate_and_store(biased, share_with_vector=True)
